import numpy as np
import ml_dtypes

BF16 = ml_dtypes.bfloat16


def bf(x):
    return np.asarray(x, np.float32).astype(BF16)


def f32(x):
    return np.asarray(x, np.float32)


def f64(x):
    return np.asarray(x).astype(np.float64)


def striped(idx):
    return np.tile(idx.reshape(-1, 16).T, (8, 1))


S, D, M, P, Q, N = 4096, 128, 512, 512, 256, 2048
GAIN, BSC, EPS = 1.5, 0.7, 1e-12


def sigmoid(v):
    return 1.0 / (1.0 + np.exp(-v))


def setup_inputs():
    return {
        "table": bf(np.random.standard_normal((S, D))),
        "w1": bf(np.random.standard_normal((D, M)) / np.sqrt(D)),
        "b1": f32(BSC * np.random.standard_normal((M, 1))),
        "w2": bf(GAIN * np.random.standard_normal((M, P)) / np.sqrt(M)),
        "b2": f32(BSC * np.random.standard_normal((P, 1))),
        "w3": bf(GAIN * np.random.standard_normal((P, Q)) / np.sqrt(P)),
        "b3": f32(BSC * np.random.standard_normal((Q, 1))),
        "path_forces": f32(np.random.uniform(size=(N, N))),
        "offs": striped(np.random.permutation(S)[:N]),
    }


def reference(table, w1, b1, w2, b2, w3, b3, path_forces, offs):
    idx = offs[:16].T.reshape(-1)
    h1 = np.tanh(f64(w1).T @ f64(table)[idx].T + f64(b1))
    h2 = np.tanh(f64(w2).T @ h1 + f64(b2))
    feats = sigmoid(f64(w3).T @ h2 + f64(b3))
    sq = np.sum(feats * feats, axis=0)
    d2 = sq[:, None] + sq[None, :] - 2.0 * (feats.T @ feats)
    dist = np.sqrt(np.maximum(d2, EPS))
    return dist * (1.0 - np.eye(N)) * f64(path_forces)

@@ -1,0 +1,169 @@
+import concourse.mybir as mybir
+from concourse.masks import make_identity
+
+BF16, F32, U16 = mybir.dt.bfloat16, mybir.dt.float32, mybir.dt.uint16
+FUNC = mybir.ActivationFunctionType
+ALU = mybir.AluOpType
+
+LANES = 128
+STORE = 4096
+FEAT = 128
+HID1, HID2, CODE = 512, 512, 256
+N = 2048
+PIECE = 512
+EPS = 1e-12
+
+PIECES = N // PIECE
+ROW_BLOCKS = N // LANES
+STORE_BLOCKS = STORE // LANES
+BLOCKS_A_BANK = 8
+
+FLOPS = 2 * N * (FEAT * HID1 + HID1 * HID2 + HID2 * CODE + N * CODE)
+
+
+def tile_controencodnet_b_kernel(tc, table, w1, b1, w2, b2, w3, b3, path_forces, offs, out):
+    nc = tc.nc
+    with (
+        tc.tile_pool(name="held", bufs=1) as held,
+        tc.tile_pool(name="weighting", bufs=ROW_BLOCKS) as weighting,
+        tc.psum_pool(name="psum", bufs=8) as psum,
+    ):
+        offsets = held.tile([LANES, N // 16], U16, name="offsets")
+        nc.sync.dma_start(offsets[:], offs)
+
+        identity_bf16 = held.tile([LANES, LANES], BF16, name="identity_bf16")
+        make_identity(nc, identity_bf16[:])
+        identity_f32 = held.tile([LANES, LANES], F32, name="identity_f32")
+        make_identity(nc, identity_f32[:])
+        ones_f32 = held.tile([LANES, LANES], F32, name="ones_f32")
+        nc.vector.memset(ones_f32[:], 1.0)
+
+        table_cols = held.tile([FEAT, STORE], BF16, name="table_cols")
+        w1_sb = held.tile([FEAT, HID1], BF16, name="w1_sb")
+        w2_sb = held.tile([LANES, HID1 // LANES, HID2], BF16, name="w2_sb")
+        w3_sb = held.tile([LANES, HID2 // LANES, CODE], BF16, name="w3_sb")
+        bias_rows = held.tile([LANES, LANES], F32, name="bias_rows")
+        bias_cols = held.tile([LANES, 10], F32, name="bias_cols")
+        feats = held.tile([LANES, CODE // LANES, N], BF16, name="feats")
+        sq_row = held.tile([LANES, N], F32, name="sq_row")
+        sq_col = held.tile([LANES, ROW_BLOCKS], F32, name="sq_col")
+
+        with tc.tile_pool(name="encode", bufs=1) as encode, tc.tile_pool(name="squares", bufs=2) as squares:
+            table_rows = encode.tile([LANES, STORE_BLOCKS, FEAT], BF16, name="table_rows")
+            table_blocks = table.rearrange("(b p) d -> p b d", p=LANES)
+            for first in range(0, STORE_BLOCKS, BLOCKS_A_BANK):
+                nc.sync.dma_start(
+                    table_rows[:, first : first + BLOCKS_A_BANK, :],
+                    table_blocks[:, first : first + BLOCKS_A_BANK, :],
+                )
+            nc.sync.dma_start(w1_sb[:], w1)
+            nc.vector.memset(bias_rows[:], 0.0)
+            nc.sync.dma_start(bias_rows[0:4, :], b1.rearrange("(k p) one -> k (p one)", p=LANES))
+            nc.sync.dma_start(bias_rows[4:8, :], b2.rearrange("(k p) one -> k (p one)", p=LANES))
+            nc.sync.dma_start(bias_rows[8:10, :], b3.rearrange("(k p) one -> k (p one)", p=LANES))
+            nc.sync.dma_start(w2_sb[:], w2.rearrange("(k p) n -> p k n", p=LANES))
+            nc.sync.dma_start(w3_sb[:], w3.rearrange("(k p) n -> p k n", p=LANES))
+            weights_of_row = []
+            for r in range(ROW_BLOCKS):
+                path = weighting.tile([LANES, N], F32, name="path")
+                nc.sync.dma_start(path[:], path_forces[r * LANES : (r + 1) * LANES, :])
+                nc.gpsimd.affine_select(
+                    out=path[:, r * LANES : (r + 1) * LANES],
+                    in_=path[:, r * LANES : (r + 1) * LANES],
+                    compare_op=ALU.not_equal,
+                    fill=0.0,
+                    base=0,
+                    pattern=[[-1, LANES]],
+                    channel_multiplier=1,
+                )
+                weights_of_row.append(path)
+
+            for first in range(0, STORE_BLOCKS, BLOCKS_A_BANK):
+                turned = psum.tile([LANES, BLOCKS_A_BANK * LANES], BF16, name="turned", tag="bank")
+                for b in range(BLOCKS_A_BANK):
+                    nc.tensor.transpose(
+                        turned[:, b * LANES : (b + 1) * LANES], table_rows[:, first + b, :], identity_bf16[:]
+                    )
+                nc.vector.tensor_copy(table_cols[:, first * LANES : (first + BLOCKS_A_BANK) * LANES], turned[:])
+
+            bias_turned = psum.tile([LANES, LANES], F32, name="bias_turned", tag="bank")
+            nc.tensor.transpose(bias_turned[:], bias_rows[:], identity_f32[:])
+            nc.vector.tensor_copy(bias_cols[:], bias_turned[:, 0:10])
+            b1_cols, b2_cols, b3_cols = bias_cols[:, 0:4], bias_cols[:, 4:8], bias_cols[:, 8:10]
+
+            h1 = encode.tile([LANES, HID1 // LANES, N], BF16, name="h1")
+            for c in range(PIECES):
+                looked_up = table_cols[:].indirect(offsets[:, c * (PIECE // 16) : (c + 1) * (PIECE // 16)])
+                for m in range(HID1 // LANES):
+                    acc = psum.tile([LANES, PIECE], F32, name="acc", tag="bank")
+                    nc.tensor.matmul(acc[:], w1_sb[:, m * LANES : (m + 1) * LANES], looked_up, start=True, stop=True)
+                    nc.scalar.activation(
+                        h1[:, m, c * PIECE : (c + 1) * PIECE], acc[:], FUNC.Tanh, bias=b1_cols[:, m : m + 1]
+                    )
+
+            h2 = encode.tile([LANES, HID2 // LANES, N], BF16, name="h2")
+            for c in range(PIECES):
+                for m in range(HID2 // LANES):
+                    acc = psum.tile([LANES, PIECE], F32, name="acc", tag="bank")
+                    for k in range(HID1 // LANES):
+                        nc.tensor.matmul(
+                            acc[:],
+                            w2_sb[:, k, m * LANES : (m + 1) * LANES],
+                            h1[:, k, c * PIECE : (c + 1) * PIECE],
+                            start=(k == 0),
+                            stop=(k == HID1 // LANES - 1),
+                        )
+                    nc.scalar.activation(
+                        h2[:, m, c * PIECE : (c + 1) * PIECE], acc[:], FUNC.Tanh, bias=b2_cols[:, m : m + 1]
+                    )
+
+            for c in range(PIECES):
+                cols = slice(c * PIECE, (c + 1) * PIECE)
+                for m in range(CODE // LANES):
+                    acc = psum.tile([LANES, PIECE], F32, name="acc", tag="bank")
+                    for k in range(HID2 // LANES):
+                        nc.tensor.matmul(
+                            acc[:],
+                            w3_sb[:, k, m * LANES : (m + 1) * LANES],
+                            h2[:, k, cols],
+                            start=(k == 0),
+                            stop=(k == HID2 // LANES - 1),
+                        )
+                    nc.scalar.activation(feats[:, m, cols], acc[:], FUNC.Sigmoid, bias=b3_cols[:, m : m + 1])
+                squared = squares.tile([LANES, CODE // LANES, PIECE], F32, name="squared")
+                nc.vector.tensor_tensor(squared[:], feats[:, :, cols], feats[:, :, cols], ALU.mult)
+                both = squares.tile([LANES, PIECE], F32, name="both")
+                nc.vector.tensor_tensor(both[:], squared[:, 0, :], squared[:, 1, :], ALU.add)
+                summed = psum.tile([LANES, PIECE], F32, name="summed", tag="bank")
+                nc.tensor.matmul(summed[:], ones_f32[:], both[:], start=True, stop=True)
+                nc.vector.tensor_copy(sq_row[:, cols], summed[:])
+                blocks = PIECE // LANES
+                diagonal = squares.tile([LANES, blocks, LANES], F32, name="diagonal")
+                nc.vector.tensor_tensor(
+                    diagonal[:],
+                    sq_row[:, cols].rearrange("p (r j) -> p r j", j=LANES),
+                    identity_f32[:].unsqueeze(1).to_broadcast([LANES, blocks, LANES]),
+                    ALU.mult,
+                )
+                nc.vector.reduce_sum(sq_col[:, c * blocks : (c + 1) * blocks], diagonal[:], axis=mybir.AxisListType.X)
+
+        with tc.tile_pool(name="work", bufs=4) as work:
+            for r in range(ROW_BLOCKS):
+                rows = slice(r * LANES, (r + 1) * LANES)
+                dist = work.tile([LANES, N], F32, name="dist")
+                for c in range(PIECES):
+                    cols = slice(c * PIECE, (c + 1) * PIECE)
+                    dots = psum.tile([LANES, PIECE], F32, name="dots", tag="bank")
+                    for k in range(CODE // LANES):
+                        nc.tensor.matmul(
+                            dots[:], feats[:, k, rows], feats[:, k, cols], start=(k == 0), stop=(k == CODE // LANES - 1)
+                        )
+                    nc.vector.scalar_tensor_tensor(
+                        out=dist[:, cols], in0=dots[:], scalar=-2.0, in1=sq_row[:, cols], op0=ALU.mult, op1=ALU.add
+                    )
+                nc.gpsimd.tensor_scalar(
+                    out=dist[:], in0=dist[:], scalar1=sq_col[:, r : r + 1], scalar2=EPS, op0=ALU.add, op1=ALU.max
+                )
+                nc.scalar.activation(dist[:], dist[:], FUNC.Sqrt)
+                nc.vector.tensor_tensor(dist[:], dist[:], weights_of_row[r][:], ALU.mult)
+                nc.sync.dma_start(out[rows, :], dist[:])

@@ -47,6 +47,9 @@ def tile_controencodnet_b_kernel(tc, table, w1, b1, w2, b2, w3, b3, path_forces,
         feats = held.tile([LANES, CODE // LANES, N], BF16, name="feats")
         sq_row = held.tile([LANES, N], F32, name="sq_row")
         sq_col = held.tile([LANES, ROW_BLOCKS], F32, name="sq_col")
+        sq_col_less_eps = held.tile([LANES, ROW_BLOCKS], F32, name="sq_col_less_eps")
+        eps_col = held.tile([LANES, 1], F32, name="eps_col")
+        nc.vector.memset(eps_col[:], EPS)
 
         with tc.tile_pool(name="encode", bufs=1) as encode, tc.tile_pool(name="squares", bufs=2) as squares:
             table_rows = encode.tile([LANES, STORE_BLOCKS, FEAT], BF16, name="table_rows")
@@ -146,24 +149,46 @@ def tile_controencodnet_b_kernel(tc, table, w1, b1, w2, b2, w3, b3, path_forces,
                     ALU.mult,
                 )
                 nc.vector.reduce_sum(sq_col[:, c * blocks : (c + 1) * blocks], diagonal[:], axis=mybir.AxisListType.X)
+            nc.vector.tensor_scalar_sub(sq_col_less_eps[:], sq_col[:], EPS)
 
-        with tc.tile_pool(name="work", bufs=4) as work:
+        with tc.tile_pool(name="distances", bufs=1) as distances:
+            direct_of_row = []
             for r in range(ROW_BLOCKS):
                 rows = slice(r * LANES, (r + 1) * LANES)
-                dist = work.tile([LANES, N], F32, name="dist")
-                for c in range(PIECES):
-                    cols = slice(c * PIECE, (c + 1) * PIECE)
+                first = r * LANES
+                path = weights_of_row[r]
+                direct = distances.tile([LANES, N - first], F32, name=f"direct{r}")
+                direct_of_row.append(direct)
+                for lo in range(first - first % PIECE, N, PIECE):
+                    lo, hi = max(lo, first), lo + PIECE
                     dots = psum.tile([LANES, PIECE], F32, name="dots", tag="bank")
                     for k in range(CODE // LANES):
                         nc.tensor.matmul(
-                            dots[:], feats[:, k, rows], feats[:, k, cols], start=(k == 0), stop=(k == CODE // LANES - 1)
+                            dots[:, : hi - lo],
+                            feats[:, k, rows],
+                            feats[:, k, lo:hi],
+                            start=(k == 0),
+                            stop=(k == CODE // LANES - 1),
                         )
                     nc.vector.scalar_tensor_tensor(
-                        out=dist[:, cols], in0=dots[:], scalar=-2.0, in1=sq_row[:, cols], op0=ALU.mult, op1=ALU.add
+                        out=direct[:, lo - first : hi - first],
+                        in0=dots[:, : hi - lo],
+                        scalar=-2.0,
+                        in1=sq_row[:, lo:hi],
+                        op0=ALU.mult,
+                        op1=ALU.add,
                     )
-                nc.gpsimd.tensor_scalar(
-                    out=dist[:], in0=dist[:], scalar1=sq_col[:, r : r + 1], scalar2=EPS, op0=ALU.add, op1=ALU.max
-                )
-                nc.scalar.activation(dist[:], dist[:], FUNC.Sqrt)
-                nc.vector.tensor_tensor(dist[:], dist[:], weights_of_row[r][:], ALU.mult)
-                nc.sync.dma_start(out[rows, :], dist[:])
+                nc.scalar.activation(direct[:], direct[:], FUNC.Relu, bias=sq_col_less_eps[:, r : r + 1])
+                nc.scalar.activation(direct[:], direct[:], FUNC.Sqrt, bias=eps_col[:])
+                nc.gpsimd.tensor_tensor(path[:, first:], direct[:], path[:, first:], ALU.mult)
+                for lo in range(0, first, PIECE):
+                    hi = min(lo + PIECE, first)
+                    mirrored = psum.tile([LANES, PIECE], F32, name="mirrored", tag="bank")
+                    for s in range(lo // LANES, hi // LANES):
+                        nc.tensor.transpose(
+                            mirrored[:, s * LANES - lo : (s + 1) * LANES - lo],
+                            direct_of_row[s][:, first - s * LANES : first - s * LANES + LANES],
+                            identity_f32[:],
+                        )
+                    nc.vector.tensor_tensor(path[:, lo:hi], mirrored[:, : hi - lo], path[:, lo:hi], ALU.mult)
+                nc.sync.dma_start(out[rows, :], path[:])

@@ -16,7 +16,9 @@ EPS = 1e-12
 PIECES = N // PIECE
 ROW_BLOCKS = N // LANES
 STORE_BLOCKS = STORE // LANES
-BLOCKS_A_BANK = 8
+BLOCKS_A_PIECE = PIECE // LANES
+TURNS_A_BANK = 8
+PSUM_BANKS = 8
 
 FLOPS = 2 * N * (FEAT * HID1 + HID1 * HID2 + HID2 * CODE + N * CODE)
 
@@ -26,7 +28,7 @@ def tile_controencodnet_b_kernel(tc, table, w1, b1, w2, b2, w3, b3, path_forces,
     with (
         tc.tile_pool(name="held", bufs=1) as held,
         tc.tile_pool(name="weighting", bufs=ROW_BLOCKS) as weighting,
-        tc.psum_pool(name="psum", bufs=8) as psum,
+        tc.psum_pool(name="psum", bufs=PSUM_BANKS) as psum,
     ):
         offsets = held.tile([LANES, N // 16], U16, name="offsets")
         nc.sync.dma_start(offsets[:], offs)
@@ -37,6 +39,8 @@ def tile_controencodnet_b_kernel(tc, table, w1, b1, w2, b2, w3, b3, path_forces,
         make_identity(nc, identity_f32[:])
         ones_f32 = held.tile([LANES, LANES], F32, name="ones_f32")
         nc.vector.memset(ones_f32[:], 1.0)
+        eps_col = held.tile([LANES, 1], F32, name="eps_col")
+        nc.vector.memset(eps_col[:], EPS)
 
         table_cols = held.tile([FEAT, STORE], BF16, name="table_cols")
         w1_sb = held.tile([FEAT, HID1], BF16, name="w1_sb")
@@ -48,17 +52,12 @@ def tile_controencodnet_b_kernel(tc, table, w1, b1, w2, b2, w3, b3, path_forces,
         sq_row = held.tile([LANES, N], F32, name="sq_row")
         sq_col = held.tile([LANES, ROW_BLOCKS], F32, name="sq_col")
         sq_col_less_eps = held.tile([LANES, ROW_BLOCKS], F32, name="sq_col_less_eps")
-        eps_col = held.tile([LANES, 1], F32, name="eps_col")
-        nc.vector.memset(eps_col[:], EPS)
 
         with tc.tile_pool(name="encode", bufs=1) as encode, tc.tile_pool(name="squares", bufs=2) as squares:
             table_rows = encode.tile([LANES, STORE_BLOCKS, FEAT], BF16, name="table_rows")
             table_blocks = table.rearrange("(b p) d -> p b d", p=LANES)
-            for first in range(0, STORE_BLOCKS, BLOCKS_A_BANK):
-                nc.sync.dma_start(
-                    table_rows[:, first : first + BLOCKS_A_BANK, :],
-                    table_blocks[:, first : first + BLOCKS_A_BANK, :],
-                )
+            for b in range(0, STORE_BLOCKS, TURNS_A_BANK):
+                nc.sync.dma_start(table_rows[:, b : b + TURNS_A_BANK, :], table_blocks[:, b : b + TURNS_A_BANK, :])
             nc.sync.dma_start(w1_sb[:], w1)
             nc.vector.memset(bias_rows[:], 0.0)
             nc.sync.dma_start(bias_rows[0:4, :], b1.rearrange("(k p) one -> k (p one)", p=LANES))
@@ -66,7 +65,7 @@ def tile_controencodnet_b_kernel(tc, table, w1, b1, w2, b2, w3, b3, path_forces,
             nc.sync.dma_start(bias_rows[8:10, :], b3.rearrange("(k p) one -> k (p one)", p=LANES))
             nc.sync.dma_start(w2_sb[:], w2.rearrange("(k p) n -> p k n", p=LANES))
             nc.sync.dma_start(w3_sb[:], w3.rearrange("(k p) n -> p k n", p=LANES))
-            weights_of_row = []
+            path_of_row = []
             for r in range(ROW_BLOCKS):
                 path = weighting.tile([LANES, N], F32, name="path")
                 nc.sync.dma_start(path[:], path_forces[r * LANES : (r + 1) * LANES, :])
@@ -79,15 +78,13 @@ def tile_controencodnet_b_kernel(tc, table, w1, b1, w2, b2, w3, b3, path_forces,
                     pattern=[[-1, LANES]],
                     channel_multiplier=1,
                 )
-                weights_of_row.append(path)
+                path_of_row.append(path)
 
-            for first in range(0, STORE_BLOCKS, BLOCKS_A_BANK):
-                turned = psum.tile([LANES, BLOCKS_A_BANK * LANES], BF16, name="turned", tag="bank")
-                for b in range(BLOCKS_A_BANK):
-                    nc.tensor.transpose(
-                        turned[:, b * LANES : (b + 1) * LANES], table_rows[:, first + b, :], identity_bf16[:]
-                    )
-                nc.vector.tensor_copy(table_cols[:, first * LANES : (first + BLOCKS_A_BANK) * LANES], turned[:])
+            for b in range(0, STORE_BLOCKS, TURNS_A_BANK):
+                turned = psum.tile([LANES, TURNS_A_BANK * LANES], BF16, name="turned", tag="bank")
+                for t in range(TURNS_A_BANK):
+                    nc.tensor.transpose(turned[:, t * LANES : (t + 1) * LANES], table_rows[:, b + t, :], identity_bf16[:])
+                nc.vector.tensor_copy(table_cols[:, b * LANES : (b + TURNS_A_BANK) * LANES], turned[:])
 
             bias_turned = psum.tile([LANES, LANES], F32, name="bias_turned", tag="bank")
             nc.tensor.transpose(bias_turned[:], bias_rows[:], identity_f32[:])
@@ -96,71 +93,73 @@ def tile_controencodnet_b_kernel(tc, table, w1, b1, w2, b2, w3, b3, path_forces,
 
             h1 = encode.tile([LANES, HID1 // LANES, N], BF16, name="h1")
             for c in range(PIECES):
+                cols = slice(c * PIECE, (c + 1) * PIECE)
                 looked_up = table_cols[:].indirect(offsets[:, c * (PIECE // 16) : (c + 1) * (PIECE // 16)])
                 for m in range(HID1 // LANES):
                     acc = psum.tile([LANES, PIECE], F32, name="acc", tag="bank")
                     nc.tensor.matmul(acc[:], w1_sb[:, m * LANES : (m + 1) * LANES], looked_up, start=True, stop=True)
-                    nc.scalar.activation(
-                        h1[:, m, c * PIECE : (c + 1) * PIECE], acc[:], FUNC.Tanh, bias=b1_cols[:, m : m + 1]
-                    )
+                    nc.scalar.activation(h1[:, m, cols], acc[:], FUNC.Tanh, bias=b1_cols[:, m : m + 1])
 
             h2 = encode.tile([LANES, HID2 // LANES, N], BF16, name="h2")
             for c in range(PIECES):
+                cols = slice(c * PIECE, (c + 1) * PIECE)
                 for m in range(HID2 // LANES):
                     acc = psum.tile([LANES, PIECE], F32, name="acc", tag="bank")
                     for k in range(HID1 // LANES):
                         nc.tensor.matmul(
                             acc[:],
                             w2_sb[:, k, m * LANES : (m + 1) * LANES],
-                            h1[:, k, c * PIECE : (c + 1) * PIECE],
+                            h1[:, k, cols],
                             start=(k == 0),
                             stop=(k == HID1 // LANES - 1),
                         )
-                    nc.scalar.activation(
-                        h2[:, m, c * PIECE : (c + 1) * PIECE], acc[:], FUNC.Tanh, bias=b2_cols[:, m : m + 1]
-                    )
+                    nc.scalar.activation(h2[:, m, cols], acc[:], FUNC.Tanh, bias=b2_cols[:, m : m + 1])
 
-            for c in range(PIECES):
-                cols = slice(c * PIECE, (c + 1) * PIECE)
-                for m in range(CODE // LANES):
-                    acc = psum.tile([LANES, PIECE], F32, name="acc", tag="bank")
-                    for k in range(HID2 // LANES):
-                        nc.tensor.matmul(
-                            acc[:],
-                            w3_sb[:, k, m * LANES : (m + 1) * LANES],
-                            h2[:, k, cols],
-                            start=(k == 0),
-                            stop=(k == HID2 // LANES - 1),
-                        )
-                    nc.scalar.activation(feats[:, m, cols], acc[:], FUNC.Sigmoid, bias=b3_cols[:, m : m + 1])
-                squared = squares.tile([LANES, CODE // LANES, PIECE], F32, name="squared")
-                nc.vector.tensor_tensor(squared[:], feats[:, :, cols], feats[:, :, cols], ALU.mult)
-                both = squares.tile([LANES, PIECE], F32, name="both")
-                nc.vector.tensor_tensor(both[:], squared[:, 0, :], squared[:, 1, :], ALU.add)
-                summed = psum.tile([LANES, PIECE], F32, name="summed", tag="bank")
-                nc.tensor.matmul(summed[:], ones_f32[:], both[:], start=True, stop=True)
-                nc.vector.tensor_copy(sq_row[:, cols], summed[:])
-                blocks = PIECE // LANES
-                diagonal = squares.tile([LANES, blocks, LANES], F32, name="diagonal")
-                nc.vector.tensor_tensor(
-                    diagonal[:],
-                    sq_row[:, cols].rearrange("p (r j) -> p r j", j=LANES),
-                    identity_f32[:].unsqueeze(1).to_broadcast([LANES, blocks, LANES]),
-                    ALU.mult,
-                )
-                nc.vector.reduce_sum(sq_col[:, c * blocks : (c + 1) * blocks], diagonal[:], axis=mybir.AxisListType.X)
-            nc.vector.tensor_scalar_sub(sq_col_less_eps[:], sq_col[:], EPS)
+            both_of_piece = []
+            for c in range(PIECES + 1):
+                if c < PIECES:
+                    cols = slice(c * PIECE, (c + 1) * PIECE)
+                    squared = squares.tile([LANES, CODE // LANES, PIECE], F32, name="squared")
+                    for m in range(CODE // LANES):
+                        acc = psum.tile([LANES, PIECE], F32, name="acc", tag="bank")
+                        for k in range(HID2 // LANES):
+                            nc.tensor.matmul(
+                                acc[:],
+                                w3_sb[:, k, m * LANES : (m + 1) * LANES],
+                                h2[:, k, cols],
+                                start=(k == 0),
+                                stop=(k == HID2 // LANES - 1),
+                            )
+                        nc.scalar.activation(feats[:, m, cols], acc[:], FUNC.Sigmoid, bias=b3_cols[:, m : m + 1])
+                        nc.vector.tensor_tensor(squared[:, m, :], feats[:, m, cols], feats[:, m, cols], ALU.mult)
+                    both = squares.tile([LANES, PIECE], F32, name="both")
+                    nc.vector.tensor_tensor(both[:], squared[:, 0, :], squared[:, 1, :], ALU.add)
+                    both_of_piece.append(both)
+                if c > 0:
+                    cols = slice((c - 1) * PIECE, c * PIECE)
+                    blocks = slice((c - 1) * BLOCKS_A_PIECE, c * BLOCKS_A_PIECE)
+                    summed = psum.tile([LANES, PIECE], F32, name="summed", tag="bank")
+                    nc.tensor.matmul(summed[:], ones_f32[:], both_of_piece[c - 1][:], start=True, stop=True)
+                    nc.vector.tensor_copy(sq_row[:, cols], summed[:])
+                    diagonal = squares.tile([LANES, BLOCKS_A_PIECE, LANES], F32, name="diagonal")
+                    nc.vector.tensor_tensor(
+                        diagonal[:],
+                        sq_row[:, cols].rearrange("p (r j) -> p r j", j=LANES),
+                        identity_f32[:].unsqueeze(1).to_broadcast([LANES, BLOCKS_A_PIECE, LANES]),
+                        ALU.mult,
+                    )
+                    nc.vector.reduce_sum(sq_col[:, blocks], diagonal[:], axis=mybir.AxisListType.X)
+                    nc.vector.tensor_scalar_sub(sq_col_less_eps[:, blocks], sq_col[:, blocks], EPS)
 
         with tc.tile_pool(name="distances", bufs=1) as distances:
             direct_of_row = []
             for r in range(ROW_BLOCKS):
                 rows = slice(r * LANES, (r + 1) * LANES)
                 first = r * LANES
-                path = weights_of_row[r]
                 direct = distances.tile([LANES, N - first], F32, name=f"direct{r}")
                 direct_of_row.append(direct)
-                for lo in range(first - first % PIECE, N, PIECE):
-                    lo, hi = max(lo, first), lo + PIECE
+                for c in range(first // PIECE, PIECES):
+                    lo, hi = max(first, c * PIECE), (c + 1) * PIECE
                     dots = psum.tile([LANES, PIECE], F32, name="dots", tag="bank")
                     for k in range(CODE // LANES):
                         nc.tensor.matmul(
@@ -180,7 +179,12 @@ def tile_controencodnet_b_kernel(tc, table, w1, b1, w2, b2, w3, b3, path_forces,
                     )
                 nc.scalar.activation(direct[:], direct[:], FUNC.Relu, bias=sq_col_less_eps[:, r : r + 1])
                 nc.scalar.activation(direct[:], direct[:], FUNC.Sqrt, bias=eps_col[:])
+                path = path_of_row[r]
                 nc.gpsimd.tensor_tensor(path[:, first:], direct[:], path[:, first:], ALU.mult)
+
+            for r in range(ROW_BLOCKS):
+                first = r * LANES
+                path = path_of_row[r]
                 for lo in range(0, first, PIECE):
                     hi = min(lo + PIECE, first)
                     mirrored = psum.tile([LANES, PIECE], F32, name="mirrored", tag="bank")
@@ -191,4 +195,4 @@ def tile_controencodnet_b_kernel(tc, table, w1, b1, w2, b2, w3, b3, path_forces,
                             identity_f32[:],
                         )
                     nc.vector.tensor_tensor(path[:, lo:hi], mirrored[:, : hi - lo], path[:, lo:hi], ALU.mult)
-                nc.sync.dma_start(out[rows, :], path[:])
+                nc.sync.dma_start(out[first : first + LANES, :], path[:])

@@ -177,7 +177,12 @@ def tile_controencodnet_b_kernel(tc, table, w1, b1, w2, b2, w3, b3, path_forces,
                         op0=ALU.mult,
                         op1=ALU.add,
                     )
-                nc.scalar.activation(direct[:], direct[:], FUNC.Relu, bias=sq_col_less_eps[:, r : r + 1])
+                    nc.scalar.activation(
+                        direct[:, lo - first : hi - first],
+                        direct[:, lo - first : hi - first],
+                        FUNC.Relu,
+                        bias=sq_col_less_eps[:, r : r + 1],
+                    )
                 nc.scalar.activation(direct[:], direct[:], FUNC.Sqrt, bias=eps_col[:])
                 path = path_of_row[r]
                 nc.gpsimd.tensor_tensor(path[:, first:], direct[:], path[:, first:], ALU.mult)

@@ -187,11 +187,14 @@ def tile_controencodnet_b_kernel(tc, table, w1, b1, w2, b2, w3, b3, path_forces,
                 path = path_of_row[r]
                 nc.gpsimd.tensor_tensor(path[:, first:], direct[:], path[:, first:], ALU.mult)
 
-            for r in range(ROW_BLOCKS):
-                first = r * LANES
-                path = path_of_row[r]
-                for lo in range(0, first, PIECE):
-                    hi = min(lo + PIECE, first)
+            for c in range(PIECES):
+                for r in range(c * BLOCKS_A_PIECE, (c + 1) * BLOCKS_A_PIECE):
+                    first = r * LANES
+                    nc.sync.dma_start(out[first : first + LANES, first:], path_of_row[r][:, first:])
+                for r in range(c * BLOCKS_A_PIECE + 1, ROW_BLOCKS):
+                    first = r * LANES
+                    lo, hi = c * PIECE, min((c + 1) * PIECE, first)
+                    path = path_of_row[r]
                     mirrored = psum.tile([LANES, PIECE], F32, name="mirrored", tag="bank")
                     for s in range(lo // LANES, hi // LANES):
                         nc.tensor.transpose(
@@ -200,4 +203,4 @@ def tile_controencodnet_b_kernel(tc, table, w1, b1, w2, b2, w3, b3, path_forces,
                             identity_f32[:],
                         )
                     nc.vector.tensor_tensor(path[:, lo:hi], mirrored[:, : hi - lo], path[:, lo:hi], ALU.mult)
-                nc.sync.dma_start(out[first : first + LANES, :], path[:])
+                    nc.sync.dma_start(out[first : first + LANES, lo:hi], path[:, lo:hi])

@@ -19,6 +19,7 @@ STORE_BLOCKS = STORE // LANES
 BLOCKS_A_PIECE = PIECE // LANES
 TURNS_A_BANK = 8
 PSUM_BANKS = 8
+GPSIMD_ROWS = ROW_BLOCKS // 2
 
 FLOPS = 2 * N * (FEAT * HID1 + HID1 * HID2 + HID2 * CODE + N * CODE)
 
@@ -184,13 +185,17 @@ def tile_controencodnet_b_kernel(tc, table, w1, b1, w2, b2, w3, b3, path_forces,
                         bias=sq_col_less_eps[:, r : r + 1],
                     )
                 nc.scalar.activation(direct[:], direct[:], FUNC.Sqrt, bias=eps_col[:])
-                path = path_of_row[r]
-                nc.gpsimd.tensor_tensor(path[:, first:], direct[:], path[:, first:], ALU.mult)
+                if r < GPSIMD_ROWS:
+                    path = path_of_row[r]
+                    nc.gpsimd.tensor_tensor(path[:, first:], direct[:], path[:, first:], ALU.mult)
 
             for c in range(PIECES):
                 for r in range(c * BLOCKS_A_PIECE, (c + 1) * BLOCKS_A_PIECE):
                     first = r * LANES
-                    nc.sync.dma_start(out[first : first + LANES, first:], path_of_row[r][:, first:])
+                    path = path_of_row[r]
+                    if r >= GPSIMD_ROWS:
+                        nc.vector.tensor_tensor(path[:, first:], direct_of_row[r][:], path[:, first:], ALU.mult)
+                    nc.sync.dma_start(out[first : first + LANES, first:], path[:, first:])
                 for r in range(c * BLOCKS_A_PIECE + 1, ROW_BLOCKS):
                     first = r * LANES
                     lo, hi = c * PIECE, min((c + 1) * PIECE, first)

@@ -19,7 +19,7 @@ STORE_BLOCKS = STORE // LANES
 BLOCKS_A_PIECE = PIECE // LANES
 TURNS_A_BANK = 8
 PSUM_BANKS = 8
-GPSIMD_ROWS = ROW_BLOCKS // 2
+DIST_TILES = 16
 
 FLOPS = 2 * N * (FEAT * HID1 + HID1 * HID2 + HID2 * CODE + N * CODE)
 
@@ -152,60 +152,61 @@ def tile_controencodnet_b_kernel(tc, table, w1, b1, w2, b2, w3, b3, path_forces,
                     nc.vector.reduce_sum(sq_col[:, blocks], diagonal[:], axis=mybir.AxisListType.X)
                     nc.vector.tensor_scalar_sub(sq_col_less_eps[:, blocks], sq_col[:, blocks], EPS)
 
-        with tc.tile_pool(name="distances", bufs=1) as distances:
-            direct_of_row = []
-            for r in range(ROW_BLOCKS):
-                rows = slice(r * LANES, (r + 1) * LANES)
-                first = r * LANES
-                direct = distances.tile([LANES, N - first], F32, name=f"direct{r}")
-                direct_of_row.append(direct)
-                for c in range(first // PIECE, PIECES):
-                    lo, hi = max(first, c * PIECE), (c + 1) * PIECE
+        with tc.tile_pool(name="distances", bufs=DIST_TILES) as distances:
+            dist_of = {}
+
+            def direct(a, c):
+                for r in range(a * BLOCKS_A_PIECE, (a + 1) * BLOCKS_A_PIECE):
+                    rows = slice(r * LANES, (r + 1) * LANES)
+                    lo, hi = max(r * LANES, c * PIECE), (c + 1) * PIECE
+                    width = hi - lo
                     dots = psum.tile([LANES, PIECE], F32, name="dots", tag="bank")
                     for k in range(CODE // LANES):
                         nc.tensor.matmul(
-                            dots[:, : hi - lo],
+                            dots[:, :width],
                             feats[:, k, rows],
                             feats[:, k, lo:hi],
                             start=(k == 0),
                             stop=(k == CODE // LANES - 1),
                         )
+                    dist = distances.tile([LANES, PIECE], F32, name="dist")
+                    dist_of[(r, c)] = (dist, lo)
                     nc.vector.scalar_tensor_tensor(
-                        out=direct[:, lo - first : hi - first],
-                        in0=dots[:, : hi - lo],
+                        out=dist[:, :width],
+                        in0=dots[:, :width],
                         scalar=-2.0,
                         in1=sq_row[:, lo:hi],
                         op0=ALU.mult,
                         op1=ALU.add,
                     )
-                    nc.scalar.activation(
-                        direct[:, lo - first : hi - first],
-                        direct[:, lo - first : hi - first],
-                        FUNC.Relu,
-                        bias=sq_col_less_eps[:, r : r + 1],
-                    )
-                nc.scalar.activation(direct[:], direct[:], FUNC.Sqrt, bias=eps_col[:])
-                if r < GPSIMD_ROWS:
+                    nc.scalar.activation(dist[:, :width], dist[:, :width], FUNC.Relu, bias=sq_col_less_eps[:, r : r + 1])
+                    nc.scalar.activation(dist[:, :width], dist[:, :width], FUNC.Sqrt, bias=eps_col[:])
                     path = path_of_row[r]
-                    nc.gpsimd.tensor_tensor(path[:, first:], direct[:], path[:, first:], ALU.mult)
+                    multiplier = nc.vector if a == c else nc.gpsimd
+                    multiplier.tensor_tensor(path[:, lo:hi], dist[:, :width], path[:, lo:hi], ALU.mult)
+                    nc.sync.dma_start(out[rows, lo:hi], path[:, lo:hi])
 
-            for c in range(PIECES):
+            def mirrored(a, c):
                 for r in range(c * BLOCKS_A_PIECE, (c + 1) * BLOCKS_A_PIECE):
-                    first = r * LANES
-                    path = path_of_row[r]
-                    if r >= GPSIMD_ROWS:
-                        nc.vector.tensor_tensor(path[:, first:], direct_of_row[r][:], path[:, first:], ALU.mult)
-                    nc.sync.dma_start(out[first : first + LANES, first:], path[:, first:])
-                for r in range(c * BLOCKS_A_PIECE + 1, ROW_BLOCKS):
-                    first = r * LANES
-                    lo, hi = c * PIECE, min((c + 1) * PIECE, first)
-                    path = path_of_row[r]
-                    mirrored = psum.tile([LANES, PIECE], F32, name="mirrored", tag="bank")
-                    for s in range(lo // LANES, hi // LANES):
+                    sources = [s for s in range(a * BLOCKS_A_PIECE, (a + 1) * BLOCKS_A_PIECE) if s < r]
+                    if not sources:
+                        continue
+                    lo, hi = a * PIECE, a * PIECE + len(sources) * LANES
+                    turned_back = psum.tile([LANES, PIECE], F32, name="turned_back", tag="bank")
+                    for s in sources:
+                        dist, first = dist_of[(s, c)]
                         nc.tensor.transpose(
-                            mirrored[:, s * LANES - lo : (s + 1) * LANES - lo],
-                            direct_of_row[s][:, first - s * LANES : first - s * LANES + LANES],
+                            turned_back[:, s * LANES - lo : (s + 1) * LANES - lo],
+                            dist[:, r * LANES - first : (r + 1) * LANES - first],
                             identity_f32[:],
                         )
-                    nc.vector.tensor_tensor(path[:, lo:hi], mirrored[:, : hi - lo], path[:, lo:hi], ALU.mult)
-                    nc.sync.dma_start(out[first : first + LANES, lo:hi], path[:, lo:hi])
+                    path = path_of_row[r]
+                    nc.vector.tensor_tensor(path[:, lo:hi], turned_back[:, : hi - lo], path[:, lo:hi], ALU.mult)
+                    nc.sync.dma_start(out[r * LANES : (r + 1) * LANES, lo:hi], path[:, lo:hi])
+
+            squares_in_order = [(a, c) for c in range(PIECES) for a in range(c + 1)]
+            for n, (a, c) in enumerate(squares_in_order):
+                direct(a, c)
+                if n > 0:
+                    mirrored(*squares_in_order[n - 1])
+            mirrored(*squares_in_order[-1])

@@ -28,7 +28,7 @@ def tile_controencodnet_b_kernel(tc, table, w1, b1, w2, b2, w3, b3, path_forces,
     nc = tc.nc
     with (
         tc.tile_pool(name="held", bufs=1) as held,
-        tc.tile_pool(name="weighting", bufs=ROW_BLOCKS) as weighting,
+        tc.tile_pool(name="weighting", bufs=1) as weighting,
         tc.psum_pool(name="psum", bufs=PSUM_BANKS) as psum,
     ):
         offsets = held.tile([LANES, N // 16], U16, name="offsets")
@@ -49,13 +49,14 @@ def tile_controencodnet_b_kernel(tc, table, w1, b1, w2, b2, w3, b3, path_forces,
         w3_sb = held.tile([LANES, HID2 // LANES, CODE], BF16, name="w3_sb")
         bias_rows = held.tile([LANES, LANES], F32, name="bias_rows")
         bias_cols = held.tile([LANES, 10], F32, name="bias_cols")
+        h1 = held.tile([LANES, HID1 // LANES, N], BF16, name="h1")
         feats = held.tile([LANES, CODE // LANES, N], BF16, name="feats")
         sq_row = held.tile([LANES, N], F32, name="sq_row")
         sq_col = held.tile([LANES, ROW_BLOCKS], F32, name="sq_col")
         sq_col_less_eps = held.tile([LANES, ROW_BLOCKS], F32, name="sq_col_less_eps")
 
-        with tc.tile_pool(name="encode", bufs=1) as encode, tc.tile_pool(name="squares", bufs=2) as squares:
-            table_rows = encode.tile([LANES, STORE_BLOCKS, FEAT], BF16, name="table_rows")
+        with tc.tile_pool(name="loading", bufs=1) as loading:
+            table_rows = loading.tile([LANES, STORE_BLOCKS, FEAT], BF16, name="table_rows")
             table_blocks = table.rearrange("(b p) d -> p b d", p=LANES)
             for b in range(0, STORE_BLOCKS, TURNS_A_BANK):
                 nc.sync.dma_start(table_rows[:, b : b + TURNS_A_BANK, :], table_blocks[:, b : b + TURNS_A_BANK, :])
@@ -66,10 +67,11 @@ def tile_controencodnet_b_kernel(tc, table, w1, b1, w2, b2, w3, b3, path_forces,
             nc.sync.dma_start(bias_rows[8:10, :], b3.rearrange("(k p) one -> k (p one)", p=LANES))
             nc.sync.dma_start(w2_sb[:], w2.rearrange("(k p) n -> p k n", p=LANES))
             nc.sync.dma_start(w3_sb[:], w3.rearrange("(k p) n -> p k n", p=LANES))
-            path_of_row = []
+            path_all = weighting.tile([LANES, ROW_BLOCKS, N], F32, name="path_all")
+            out_blocks = out.rearrange("(r p) j -> p r j", p=LANES)
             for r in range(ROW_BLOCKS):
-                path = weighting.tile([LANES, N], F32, name="path")
-                nc.sync.dma_start(path[:], path_forces[r * LANES : (r + 1) * LANES, :])
+                path = path_all[:, r, :]
+                nc.sync.dma_start(path, path_forces[r * LANES : (r + 1) * LANES, :])
                 nc.gpsimd.affine_select(
                     out=path[:, r * LANES : (r + 1) * LANES],
                     in_=path[:, r * LANES : (r + 1) * LANES],
@@ -79,7 +81,6 @@ def tile_controencodnet_b_kernel(tc, table, w1, b1, w2, b2, w3, b3, path_forces,
                     pattern=[[-1, LANES]],
                     channel_multiplier=1,
                 )
-                path_of_row.append(path)
 
             for b in range(0, STORE_BLOCKS, TURNS_A_BANK):
                 turned = psum.tile([LANES, TURNS_A_BANK * LANES], BF16, name="turned", tag="bank")
@@ -87,23 +88,32 @@ def tile_controencodnet_b_kernel(tc, table, w1, b1, w2, b2, w3, b3, path_forces,
                     nc.tensor.transpose(turned[:, t * LANES : (t + 1) * LANES], table_rows[:, b + t, :], identity_bf16[:])
                 nc.vector.tensor_copy(table_cols[:, b * LANES : (b + TURNS_A_BANK) * LANES], turned[:])
 
-            bias_turned = psum.tile([LANES, LANES], F32, name="bias_turned", tag="bank")
-            nc.tensor.transpose(bias_turned[:], bias_rows[:], identity_f32[:])
-            nc.vector.tensor_copy(bias_cols[:], bias_turned[:, 0:10])
-            b1_cols, b2_cols, b3_cols = bias_cols[:, 0:4], bias_cols[:, 4:8], bias_cols[:, 8:10]
+        bias_turned = psum.tile([LANES, LANES], F32, name="bias_turned", tag="bank")
+        nc.tensor.transpose(bias_turned[:], bias_rows[:], identity_f32[:])
+        nc.vector.tensor_copy(bias_cols[:], bias_turned[:, 0:10])
+        b1_cols, b2_cols, b3_cols = bias_cols[:, 0:4], bias_cols[:, 4:8], bias_cols[:, 8:10]
 
-            h1 = encode.tile([LANES, HID1 // LANES, N], BF16, name="h1")
-            for c in range(PIECES):
-                cols = slice(c * PIECE, (c + 1) * PIECE)
-                looked_up = table_cols[:].indirect(offsets[:, c * (PIECE // 16) : (c + 1) * (PIECE // 16)])
-                for m in range(HID1 // LANES):
-                    acc = psum.tile([LANES, PIECE], F32, name="acc", tag="bank")
-                    nc.tensor.matmul(acc[:], w1_sb[:, m * LANES : (m + 1) * LANES], looked_up, start=True, stop=True)
-                    nc.scalar.activation(h1[:, m, cols], acc[:], FUNC.Tanh, bias=b1_cols[:, m : m + 1])
+        for c in range(PIECES):
+            cols = slice(c * PIECE, (c + 1) * PIECE)
+            looked_up = table_cols[:].indirect(offsets[:, c * (PIECE // 16) : (c + 1) * (PIECE // 16)])
+            for m in range(HID1 // LANES):
+                acc = psum.tile([LANES, PIECE], F32, name="acc", tag="bank")
+                nc.tensor.matmul(acc[:], w1_sb[:, m * LANES : (m + 1) * LANES], looked_up, start=True, stop=True)
+                nc.scalar.activation(h1[:, m, cols], acc[:], FUNC.Tanh, bias=b1_cols[:, m : m + 1])
 
-            h2 = encode.tile([LANES, HID2 // LANES, N], BF16, name="h2")
-            for c in range(PIECES):
+        with (
+            tc.tile_pool(name="hidden", bufs=2) as hidden,
+            tc.tile_pool(name="squares", bufs=2) as squares,
+            tc.tile_pool(name="distances", bufs=DIST_TILES) as distances,
+        ):
+            h2_of_piece = {}
+            both_of_piece = {}
+            dist_of = {}
+
+            def layer2(c):
                 cols = slice(c * PIECE, (c + 1) * PIECE)
+                h2 = hidden.tile([LANES, HID2 // LANES, PIECE], BF16, name="h2")
+                h2_of_piece[c] = h2
                 for m in range(HID2 // LANES):
                     acc = psum.tile([LANES, PIECE], F32, name="acc", tag="bank")
                     for k in range(HID1 // LANES):
@@ -114,57 +124,56 @@ def tile_controencodnet_b_kernel(tc, table, w1, b1, w2, b2, w3, b3, path_forces,
                             start=(k == 0),
                             stop=(k == HID1 // LANES - 1),
                         )
-                    nc.scalar.activation(h2[:, m, cols], acc[:], FUNC.Tanh, bias=b2_cols[:, m : m + 1])
+                    nc.scalar.activation(h2[:, m, :], acc[:], FUNC.Tanh, bias=b2_cols[:, m : m + 1])
 
-            both_of_piece = []
-            for c in range(PIECES + 1):
-                if c < PIECES:
-                    cols = slice(c * PIECE, (c + 1) * PIECE)
-                    squared = squares.tile([LANES, CODE // LANES, PIECE], F32, name="squared")
-                    for m in range(CODE // LANES):
-                        acc = psum.tile([LANES, PIECE], F32, name="acc", tag="bank")
-                        for k in range(HID2 // LANES):
-                            nc.tensor.matmul(
-                                acc[:],
-                                w3_sb[:, k, m * LANES : (m + 1) * LANES],
-                                h2[:, k, cols],
-                                start=(k == 0),
-                                stop=(k == HID2 // LANES - 1),
-                            )
-                        nc.scalar.activation(feats[:, m, cols], acc[:], FUNC.Sigmoid, bias=b3_cols[:, m : m + 1])
-                        nc.vector.tensor_tensor(squared[:, m, :], feats[:, m, cols], feats[:, m, cols], ALU.mult)
-                    both = squares.tile([LANES, PIECE], F32, name="both")
-                    nc.vector.tensor_tensor(both[:], squared[:, 0, :], squared[:, 1, :], ALU.add)
-                    both_of_piece.append(both)
-                if c > 0:
-                    cols = slice((c - 1) * PIECE, c * PIECE)
-                    blocks = slice((c - 1) * BLOCKS_A_PIECE, c * BLOCKS_A_PIECE)
-                    summed = psum.tile([LANES, PIECE], F32, name="summed", tag="bank")
-                    nc.tensor.matmul(summed[:], ones_f32[:], both_of_piece[c - 1][:], start=True, stop=True)
-                    nc.vector.tensor_copy(sq_row[:, cols], summed[:])
-                    diagonal = squares.tile([LANES, BLOCKS_A_PIECE, LANES], F32, name="diagonal")
-                    nc.vector.tensor_tensor(
-                        diagonal[:],
-                        sq_row[:, cols].rearrange("p (r j) -> p r j", j=LANES),
-                        identity_f32[:].unsqueeze(1).to_broadcast([LANES, BLOCKS_A_PIECE, LANES]),
-                        ALU.mult,
-                    )
-                    nc.vector.reduce_sum(sq_col[:, blocks], diagonal[:], axis=mybir.AxisListType.X)
-                    nc.vector.tensor_scalar_sub(sq_col_less_eps[:, blocks], sq_col[:, blocks], EPS)
+            def layer3(c):
+                cols = slice(c * PIECE, (c + 1) * PIECE)
+                h2 = h2_of_piece[c]
+                squared = squares.tile([LANES, CODE // LANES, PIECE], F32, name="squared")
+                for m in range(CODE // LANES):
+                    acc = psum.tile([LANES, PIECE], F32, name="acc", tag="bank")
+                    for k in range(HID2 // LANES):
+                        nc.tensor.matmul(
+                            acc[:],
+                            w3_sb[:, k, m * LANES : (m + 1) * LANES],
+                            h2[:, k, :],
+                            start=(k == 0),
+                            stop=(k == HID2 // LANES - 1),
+                        )
+                    nc.scalar.activation(feats[:, m, cols], acc[:], FUNC.Sigmoid, bias=b3_cols[:, m : m + 1])
+                    nc.vector.tensor_tensor(squared[:, m, :], feats[:, m, cols], feats[:, m, cols], ALU.mult)
+                both = squares.tile([LANES, PIECE], F32, name="both")
+                nc.vector.tensor_tensor(both[:], squared[:, 0, :], squared[:, 1, :], ALU.add)
+                both_of_piece[c] = both
 
-        with tc.tile_pool(name="distances", bufs=DIST_TILES) as distances:
-            dist_of = {}
+            def sum_squares(c):
+                cols = slice(c * PIECE, (c + 1) * PIECE)
+                blocks = slice(c * BLOCKS_A_PIECE, (c + 1) * BLOCKS_A_PIECE)
+                summed = psum.tile([LANES, PIECE], F32, name="summed", tag="bank")
+                nc.tensor.matmul(summed[:], ones_f32[:], both_of_piece[c][:], start=True, stop=True)
+                nc.vector.tensor_copy(sq_row[:, cols], summed[:])
+                diagonal = squares.tile([LANES, BLOCKS_A_PIECE, LANES], F32, name="diagonal")
+                nc.vector.tensor_tensor(
+                    diagonal[:],
+                    sq_row[:, cols].rearrange("p (r j) -> p r j", j=LANES),
+                    identity_f32[:].unsqueeze(1).to_broadcast([LANES, BLOCKS_A_PIECE, LANES]),
+                    ALU.mult,
+                )
+                nc.vector.reduce_sum(sq_col[:, blocks], diagonal[:], axis=mybir.AxisListType.X)
+                nc.vector.tensor_scalar_sub(sq_col_less_eps[:, blocks], sq_col[:, blocks], EPS)
 
-            def direct(a, c):
-                for r in range(a * BLOCKS_A_PIECE, (a + 1) * BLOCKS_A_PIECE):
-                    rows = slice(r * LANES, (r + 1) * LANES)
+            def row_blocks_of(piece):
+                return range(piece * BLOCKS_A_PIECE, (piece + 1) * BLOCKS_A_PIECE)
+
+            def roots(a, c):
+                for r in row_blocks_of(a):
                     lo, hi = max(r * LANES, c * PIECE), (c + 1) * PIECE
                     width = hi - lo
                     dots = psum.tile([LANES, PIECE], F32, name="dots", tag="bank")
                     for k in range(CODE // LANES):
                         nc.tensor.matmul(
                             dots[:, :width],
-                            feats[:, k, rows],
+                            feats[:, k, r * LANES : (r + 1) * LANES],
                             feats[:, k, lo:hi],
                             start=(k == 0),
                             stop=(k == CODE // LANES - 1),
@@ -181,32 +190,60 @@ def tile_controencodnet_b_kernel(tc, table, w1, b1, w2, b2, w3, b3, path_forces,
                     )
                     nc.scalar.activation(dist[:, :width], dist[:, :width], FUNC.Relu, bias=sq_col_less_eps[:, r : r + 1])
                     nc.scalar.activation(dist[:, :width], dist[:, :width], FUNC.Sqrt, bias=eps_col[:])
-                    path = path_of_row[r]
-                    multiplier = nc.vector if a == c else nc.gpsimd
-                    multiplier.tensor_tensor(path[:, lo:hi], dist[:, :width], path[:, lo:hi], ALU.mult)
-                    nc.sync.dma_start(out[rows, lo:hi], path[:, lo:hi])
 
-            def mirrored(a, c):
-                for r in range(c * BLOCKS_A_PIECE, (c + 1) * BLOCKS_A_PIECE):
-                    sources = [s for s in range(a * BLOCKS_A_PIECE, (a + 1) * BLOCKS_A_PIECE) if s < r]
-                    if not sources:
-                        continue
-                    lo, hi = a * PIECE, a * PIECE + len(sources) * LANES
-                    turned_back = psum.tile([LANES, PIECE], F32, name="turned_back", tag="bank")
-                    for s in sources:
-                        dist, first = dist_of[(s, c)]
-                        nc.tensor.transpose(
-                            turned_back[:, s * LANES - lo : (s + 1) * LANES - lo],
-                            dist[:, r * LANES - first : (r + 1) * LANES - first],
-                            identity_f32[:],
-                        )
-                    path = path_of_row[r]
-                    nc.vector.tensor_tensor(path[:, lo:hi], turned_back[:, : hi - lo], path[:, lo:hi], ALU.mult)
-                    nc.sync.dma_start(out[r * LANES : (r + 1) * LANES, lo:hi], path[:, lo:hi])
+            def direct_products(a, c):
+                for r in row_blocks_of(a):
+                    dist, lo = dist_of[(r, c)]
+                    hi = (c + 1) * PIECE
+                    multiplier = nc.vector if hi - lo == PIECE and a == c else nc.gpsimd
+                    multiplier.tensor_tensor(path_all[:, r, lo:hi], dist[:, : hi - lo], path_all[:, r, lo:hi], ALU.mult)
 
-            squares_in_order = [(a, c) for c in range(PIECES) for a in range(c + 1)]
-            for n, (a, c) in enumerate(squares_in_order):
-                direct(a, c)
-                if n > 0:
-                    mirrored(*squares_in_order[n - 1])
-            mirrored(*squares_in_order[-1])
+            def mirrored_products(a, c):
+                for r in row_blocks_of(c):
+                    sources = [s for s in row_blocks_of(a) if s < r]
+                    if sources:
+                        lo, hi = a * PIECE, a * PIECE + len(sources) * LANES
+                        turned_back = psum.tile([LANES, PIECE], F32, name="turned_back", tag="bank")
+                        for s in sources:
+                            dist, first = dist_of[(s, c)]
+                            nc.tensor.transpose(
+                                turned_back[:, s * LANES - lo : (s + 1) * LANES - lo],
+                                dist[:, r * LANES - first : (r + 1) * LANES - first],
+                                identity_f32[:],
+                            )
+                        nc.vector.tensor_tensor(path_all[:, r, lo:hi], turned_back[:, : hi - lo], path_all[:, r, lo:hi], ALU.mult)
+                    if a == c:
+                        store(slice(r, r + 1), a)
+
+            def store(blocks, piece):
+                cols = slice(piece * PIECE, (piece + 1) * PIECE)
+                nc.sync.dma_start(out_blocks[:, blocks, cols], path_all[:, blocks, cols])
+
+            def finish(a, c):
+                direct_products(a, c)
+                if a < c:
+                    store(slice(a * BLOCKS_A_PIECE, (a + 1) * BLOCKS_A_PIECE), c)
+                mirrored_products(a, c)
+                if a < c:
+                    store(slice(c * BLOCKS_A_PIECE, (c + 1) * BLOCKS_A_PIECE), a)
+
+            layer2(0)
+            layer2(1)
+            layer3(0)
+            layer2(2)
+            layer3(1)
+            sum_squares(0)
+            layer2(3)
+            layer3(2)
+            sum_squares(1)
+            layer3(3)
+            squares_in_order = [(a, c) for c in range(PIECES) for a in range(c)] + [(c, c) for c in range(PIECES)]
+            roots(*squares_in_order[0])
+            sum_squares(2)
+            roots(*squares_in_order[1])
+            finish(*squares_in_order[0])
+            sum_squares(3)
+            for n in range(2, len(squares_in_order)):
+                roots(*squares_in_order[n])
+                finish(*squares_in_order[n - 1])
+            finish(*squares_in_order[-1])

@@ -20,6 +20,7 @@ BLOCKS_A_PIECE = PIECE // LANES
 TURNS_A_BANK = 8
 PSUM_BANKS = 8
 DIST_TILES = 16
+ROWS_A_STORE = 2
 
 FLOPS = 2 * N * (FEAT * HID1 + HID1 * HID2 + HID2 * CODE + N * CODE)
 
@@ -195,8 +196,10 @@ def tile_controencodnet_b_kernel(tc, table, w1, b1, w2, b2, w3, b3, path_forces,
                 for r in row_blocks_of(a):
                     dist, lo = dist_of[(r, c)]
                     hi = (c + 1) * PIECE
-                    multiplier = nc.vector if hi - lo == PIECE and a == c else nc.gpsimd
+                    multiplier = nc.vector if hi - lo <= PIECE // 2 else nc.gpsimd
                     multiplier.tensor_tensor(path_all[:, r, lo:hi], dist[:, : hi - lo], path_all[:, r, lo:hi], ALU.mult)
+                    if a < c and (r + 1) % ROWS_A_STORE == 0:
+                        store(slice(r + 1 - ROWS_A_STORE, r + 1), c)
 
             def mirrored_products(a, c):
                 for r in row_blocks_of(c):
@@ -214,6 +217,8 @@ def tile_controencodnet_b_kernel(tc, table, w1, b1, w2, b2, w3, b3, path_forces,
                         nc.vector.tensor_tensor(path_all[:, r, lo:hi], turned_back[:, : hi - lo], path_all[:, r, lo:hi], ALU.mult)
                     if a == c:
                         store(slice(r, r + 1), a)
+                    elif (r + 1) % ROWS_A_STORE == 0:
+                        store(slice(r + 1 - ROWS_A_STORE, r + 1), a)
 
             def store(blocks, piece):
                 cols = slice(piece * PIECE, (piece + 1) * PIECE)
@@ -221,11 +226,7 @@ def tile_controencodnet_b_kernel(tc, table, w1, b1, w2, b2, w3, b3, path_forces,
 
             def finish(a, c):
                 direct_products(a, c)
-                if a < c:
-                    store(slice(a * BLOCKS_A_PIECE, (a + 1) * BLOCKS_A_PIECE), c)
                 mirrored_products(a, c)
-                if a < c:
-                    store(slice(c * BLOCKS_A_PIECE, (c + 1) * BLOCKS_A_PIECE), a)
 
             layer2(0)
             layer2(1)

@@ -189,8 +189,19 @@ def tile_controencodnet_b_kernel(tc, table, w1, b1, w2, b2, w3, b3, path_forces,
                         op0=ALU.mult,
                         op1=ALU.add,
                     )
-                    nc.scalar.activation(dist[:, :width], dist[:, :width], FUNC.Relu, bias=sq_col_less_eps[:, r : r + 1])
-                    nc.scalar.activation(dist[:, :width], dist[:, :width], FUNC.Sqrt, bias=eps_col[:])
+                    if a < c and r % BLOCKS_A_PIECE == BLOCKS_A_PIECE - 1:
+                        nc.vector.tensor_scalar(
+                            out=dist[:, :width],
+                            in0=dist[:, :width],
+                            scalar1=sq_col[:, r : r + 1],
+                            scalar2=EPS,
+                            op0=ALU.add,
+                            op1=ALU.max,
+                        )
+                        nc.scalar.activation(dist[:, :width], dist[:, :width], FUNC.Sqrt)
+                    else:
+                        nc.scalar.activation(dist[:, :width], dist[:, :width], FUNC.Relu, bias=sq_col_less_eps[:, r : r + 1])
+                        nc.scalar.activation(dist[:, :width], dist[:, :width], FUNC.Sqrt, bias=eps_col[:])
 
             def direct_products(a, c):
                 for r in row_blocks_of(a):

@@ -53,7 +53,6 @@ def tile_controencodnet_b_kernel(tc, table, w1, b1, w2, b2, w3, b3, path_forces,
         h1 = held.tile([LANES, HID1 // LANES, N], BF16, name="h1")
         feats = held.tile([LANES, CODE // LANES, N], BF16, name="feats")
         sq_row = held.tile([LANES, N], F32, name="sq_row")
-        sq_col = held.tile([LANES, ROW_BLOCKS], F32, name="sq_col")
         sq_col_less_eps = held.tile([LANES, ROW_BLOCKS], F32, name="sq_col_less_eps")
 
         with tc.tile_pool(name="loading", bufs=1) as loading:
@@ -149,19 +148,17 @@ def tile_controencodnet_b_kernel(tc, table, w1, b1, w2, b2, w3, b3, path_forces,
 
             def sum_squares(c):
                 cols = slice(c * PIECE, (c + 1) * PIECE)
-                blocks = slice(c * BLOCKS_A_PIECE, (c + 1) * BLOCKS_A_PIECE)
                 summed = psum.tile([LANES, PIECE], F32, name="summed", tag="bank")
                 nc.tensor.matmul(summed[:], ones_f32[:], both_of_piece[c][:], start=True, stop=True)
-                nc.vector.tensor_copy(sq_row[:, cols], summed[:])
-                diagonal = squares.tile([LANES, BLOCKS_A_PIECE, LANES], F32, name="diagonal")
-                nc.vector.tensor_tensor(
-                    diagonal[:],
-                    sq_row[:, cols].rearrange("p (r j) -> p r j", j=LANES),
-                    identity_f32[:].unsqueeze(1).to_broadcast([LANES, BLOCKS_A_PIECE, LANES]),
-                    ALU.mult,
-                )
-                nc.vector.reduce_sum(sq_col[:, blocks], diagonal[:], axis=mybir.AxisListType.X)
-                nc.vector.tensor_scalar_sub(sq_col_less_eps[:, blocks], sq_col[:, blocks], EPS)
+                nc.scalar.copy(sq_row[:, cols], summed[:])
+
+            def squares_as_columns(c):
+                blocks = slice(c * BLOCKS_A_PIECE, (c + 1) * BLOCKS_A_PIECE)
+                sq_turned = psum.tile([LANES, BLOCKS_A_PIECE, LANES], F32, name="sq_turned", tag="bank")
+                for b in range(BLOCKS_A_PIECE):
+                    r = c * BLOCKS_A_PIECE + b
+                    nc.tensor.transpose(sq_turned[:, b, :], sq_row[:, r * LANES : (r + 1) * LANES], identity_f32[:])
+                nc.vector.tensor_scalar_sub(sq_col_less_eps[:, blocks].unsqueeze(2), sq_turned[:, :, 0:1], EPS)
 
             def row_blocks_of(piece):
                 return range(piece * BLOCKS_A_PIECE, (piece + 1) * BLOCKS_A_PIECE)
@@ -189,43 +186,31 @@ def tile_controencodnet_b_kernel(tc, table, w1, b1, w2, b2, w3, b3, path_forces,
                         op0=ALU.mult,
                         op1=ALU.add,
                     )
-                    if a < c and r % BLOCKS_A_PIECE == BLOCKS_A_PIECE - 1:
-                        nc.vector.tensor_scalar(
-                            out=dist[:, :width],
-                            in0=dist[:, :width],
-                            scalar1=sq_col[:, r : r + 1],
-                            scalar2=EPS,
-                            op0=ALU.add,
-                            op1=ALU.max,
-                        )
-                        nc.scalar.activation(dist[:, :width], dist[:, :width], FUNC.Sqrt)
-                    else:
-                        nc.scalar.activation(dist[:, :width], dist[:, :width], FUNC.Relu, bias=sq_col_less_eps[:, r : r + 1])
-                        nc.scalar.activation(dist[:, :width], dist[:, :width], FUNC.Sqrt, bias=eps_col[:])
+                    nc.scalar.activation(dist[:, :width], dist[:, :width], FUNC.Relu, bias=sq_col_less_eps[:, r : r + 1])
+                    nc.scalar.activation(dist[:, :width], dist[:, :width], FUNC.Sqrt, bias=eps_col[:])
 
             def direct_products(a, c):
                 for r in row_blocks_of(a):
-                    dist, lo = dist_of[(r, c)]
-                    hi = (c + 1) * PIECE
-                    multiplier = nc.vector if hi - lo <= PIECE // 2 else nc.gpsimd
-                    multiplier.tensor_tensor(path_all[:, r, lo:hi], dist[:, : hi - lo], path_all[:, r, lo:hi], ALU.mult)
+                    dist, first = dist_of[(r, c)]
+                    lo, hi = max((r + 1) * LANES, c * PIECE), (c + 1) * PIECE
+                    if lo < hi:
+                        nc.gpsimd.tensor_tensor(path_all[:, r, lo:hi], dist[:, lo - first : hi - first], path_all[:, r, lo:hi], ALU.mult)
                     if a < c and (r + 1) % ROWS_A_STORE == 0:
                         store(slice(r + 1 - ROWS_A_STORE, r + 1), c)
 
             def mirrored_products(a, c):
                 for r in row_blocks_of(c):
-                    sources = [s for s in row_blocks_of(a) if s < r]
-                    if sources:
-                        lo, hi = a * PIECE, a * PIECE + len(sources) * LANES
-                        turned_back = psum.tile([LANES, PIECE], F32, name="turned_back", tag="bank")
-                        for s in sources:
-                            dist, first = dist_of[(s, c)]
-                            nc.tensor.transpose(
-                                turned_back[:, s * LANES - lo : (s + 1) * LANES - lo],
-                                dist[:, r * LANES - first : (r + 1) * LANES - first],
-                                identity_f32[:],
-                            )
-                        nc.vector.tensor_tensor(path_all[:, r, lo:hi], turned_back[:, : hi - lo], path_all[:, r, lo:hi], ALU.mult)
+                    sources = [s for s in row_blocks_of(a) if s <= r]
+                    lo, hi = a * PIECE, a * PIECE + len(sources) * LANES
+                    turned_back = psum.tile([LANES, PIECE], F32, name="turned_back", tag="bank")
+                    for s in sources:
+                        dist, first = dist_of[(s, c)]
+                        nc.tensor.transpose(
+                            turned_back[:, s * LANES - lo : (s + 1) * LANES - lo],
+                            dist[:, r * LANES - first : (r + 1) * LANES - first],
+                            identity_f32[:],
+                        )
+                    nc.vector.tensor_tensor(path_all[:, r, lo:hi], turned_back[:, : hi - lo], path_all[:, r, lo:hi], ALU.mult)
                     if a == c:
                         store(slice(r, r + 1), a)
                     elif (r + 1) % ROWS_A_STORE == 0:
@@ -246,16 +231,22 @@ def tile_controencodnet_b_kernel(tc, table, w1, b1, w2, b2, w3, b3, path_forces,
             layer3(1)
             sum_squares(0)
             layer2(3)
+            squares_as_columns(0)
             layer3(2)
             sum_squares(1)
             layer3(3)
+            squares_as_columns(1)
             squares_in_order = [(a, c) for c in range(PIECES) for a in range(c)] + [(c, c) for c in range(PIECES)]
             roots(*squares_in_order[0])
             sum_squares(2)
             roots(*squares_in_order[1])
             finish(*squares_in_order[0])
             sum_squares(3)
-            for n in range(2, len(squares_in_order)):
+            squares_as_columns(2)
+            roots(*squares_in_order[2])
+            finish(*squares_in_order[1])
+            squares_as_columns(3)
+            for n in range(3, len(squares_in_order)):
                 roots(*squares_in_order[n])
                 finish(*squares_in_order[n - 1])
             finish(*squares_in_order[-1])

@@ -150,7 +150,7 @@ def tile_controencodnet_b_kernel(tc, table, w1, b1, w2, b2, w3, b3, path_forces,
                 cols = slice(c * PIECE, (c + 1) * PIECE)
                 summed = psum.tile([LANES, PIECE], F32, name="summed", tag="bank")
                 nc.tensor.matmul(summed[:], ones_f32[:], both_of_piece[c][:], start=True, stop=True)
-                nc.scalar.copy(sq_row[:, cols], summed[:])
+                nc.vector.tensor_copy(sq_row[:, cols], summed[:])
 
             def squares_as_columns(c):
                 blocks = slice(c * BLOCKS_A_PIECE, (c + 1) * BLOCKS_A_PIECE)
@@ -163,31 +163,40 @@ def tile_controencodnet_b_kernel(tc, table, w1, b1, w2, b2, w3, b3, path_forces,
             def row_blocks_of(piece):
                 return range(piece * BLOCKS_A_PIECE, (piece + 1) * BLOCKS_A_PIECE)
 
-            def roots(a, c):
-                for r in row_blocks_of(a):
-                    lo, hi = max(r * LANES, c * PIECE), (c + 1) * PIECE
-                    width = hi - lo
-                    dots = psum.tile([LANES, PIECE], F32, name="dots", tag="bank")
-                    for k in range(CODE // LANES):
-                        nc.tensor.matmul(
-                            dots[:, :width],
-                            feats[:, k, r * LANES : (r + 1) * LANES],
-                            feats[:, k, lo:hi],
-                            start=(k == 0),
-                            stop=(k == CODE // LANES - 1),
-                        )
-                    dist = distances.tile([LANES, PIECE], F32, name="dist")
-                    dist_of[(r, c)] = (dist, lo)
-                    nc.vector.scalar_tensor_tensor(
-                        out=dist[:, :width],
-                        in0=dots[:, :width],
-                        scalar=-2.0,
-                        in1=sq_row[:, lo:hi],
-                        op0=ALU.mult,
-                        op1=ALU.add,
+            def clamp(r, c):
+                lo, hi = max(r * LANES, c * PIECE), (c + 1) * PIECE
+                width = hi - lo
+                dots = psum.tile([LANES, PIECE], F32, name="dots", tag="bank")
+                for k in range(CODE // LANES):
+                    nc.tensor.matmul(
+                        dots[:, :width],
+                        feats[:, k, r * LANES : (r + 1) * LANES],
+                        feats[:, k, lo:hi],
+                        start=(k == 0),
+                        stop=(k == CODE // LANES - 1),
                     )
-                    nc.scalar.activation(dist[:, :width], dist[:, :width], FUNC.Relu, bias=sq_col_less_eps[:, r : r + 1])
-                    nc.scalar.activation(dist[:, :width], dist[:, :width], FUNC.Sqrt, bias=eps_col[:])
+                dist = distances.tile([LANES, PIECE], F32, name="dist")
+                dist_of[(r, c)] = (dist, lo)
+                nc.vector.scalar_tensor_tensor(
+                    out=dist[:, :width],
+                    in0=dots[:, :width],
+                    scalar=-2.0,
+                    in1=sq_row[:, lo:hi],
+                    op0=ALU.mult,
+                    op1=ALU.add,
+                )
+                nc.scalar.activation(dist[:, :width], dist[:, :width], FUNC.Relu, bias=sq_col_less_eps[:, r : r + 1])
+
+            def root(r, c):
+                dist, lo = dist_of[(r, c)]
+                width = (c + 1) * PIECE - lo
+                nc.scalar.activation(dist[:, :width], dist[:, :width], FUNC.Sqrt, bias=eps_col[:])
+
+            def roots(a, c, clamped=0):
+                for n, r in enumerate(row_blocks_of(a)):
+                    if n >= clamped:
+                        clamp(r, c)
+                    root(r, c)
 
             def direct_products(a, c):
                 for r in row_blocks_of(a):
@@ -234,10 +243,12 @@ def tile_controencodnet_b_kernel(tc, table, w1, b1, w2, b2, w3, b3, path_forces,
             squares_as_columns(0)
             layer3(2)
             sum_squares(1)
-            layer3(3)
-            squares_as_columns(1)
             squares_in_order = [(a, c) for c in range(PIECES) for a in range(c)] + [(c, c) for c in range(PIECES)]
-            roots(*squares_in_order[0])
+            first_a, first_c = squares_in_order[0]
+            clamp(row_blocks_of(first_a)[0], first_c)
+            layer3(3)
+            roots(first_a, first_c, clamped=1)
+            squares_as_columns(1)
             sum_squares(2)
             roots(*squares_in_order[1])
             finish(*squares_in_order[0])

@@ -17,7 +17,7 @@ PIECES = N // PIECE
 ROW_BLOCKS = N // LANES
 STORE_BLOCKS = STORE // LANES
 BLOCKS_A_PIECE = PIECE // LANES
-TURNS_A_BANK = 8
+TURNS_A_LOAD = 4
 PSUM_BANKS = 8
 DIST_TILES = 16
 ROWS_A_STORE = 2
@@ -33,7 +33,6 @@ def tile_controencodnet_b_kernel(tc, table, w1, b1, w2, b2, w3, b3, path_forces,
         tc.psum_pool(name="psum", bufs=PSUM_BANKS) as psum,
     ):
         offsets = held.tile([LANES, N // 16], U16, name="offsets")
-        nc.sync.dma_start(offsets[:], offs)
 
         identity_bf16 = held.tile([LANES, LANES], BF16, name="identity_bf16")
         make_identity(nc, identity_bf16[:])
@@ -58,8 +57,9 @@ def tile_controencodnet_b_kernel(tc, table, w1, b1, w2, b2, w3, b3, path_forces,
         with tc.tile_pool(name="loading", bufs=1) as loading:
             table_rows = loading.tile([LANES, STORE_BLOCKS, FEAT], BF16, name="table_rows")
             table_blocks = table.rearrange("(b p) d -> p b d", p=LANES)
-            for b in range(0, STORE_BLOCKS, TURNS_A_BANK):
-                nc.sync.dma_start(table_rows[:, b : b + TURNS_A_BANK, :], table_blocks[:, b : b + TURNS_A_BANK, :])
+            for b in range(0, STORE_BLOCKS, TURNS_A_LOAD):
+                nc.sync.dma_start(table_rows[:, b : b + TURNS_A_LOAD, :], table_blocks[:, b : b + TURNS_A_LOAD, :])
+            nc.sync.dma_start(offsets[:], offs)
             nc.sync.dma_start(w1_sb[:], w1)
             nc.vector.memset(bias_rows[:], 0.0)
             nc.sync.dma_start(bias_rows[0:4, :], b1.rearrange("(k p) one -> k (p one)", p=LANES))
@@ -82,11 +82,11 @@ def tile_controencodnet_b_kernel(tc, table, w1, b1, w2, b2, w3, b3, path_forces,
                     channel_multiplier=1,
                 )
 
-            for b in range(0, STORE_BLOCKS, TURNS_A_BANK):
-                turned = psum.tile([LANES, TURNS_A_BANK * LANES], BF16, name="turned", tag="bank")
-                for t in range(TURNS_A_BANK):
+            for b in range(0, STORE_BLOCKS, TURNS_A_LOAD):
+                turned = psum.tile([LANES, TURNS_A_LOAD * LANES], BF16, name="turned", tag="bank")
+                for t in range(TURNS_A_LOAD):
                     nc.tensor.transpose(turned[:, t * LANES : (t + 1) * LANES], table_rows[:, b + t, :], identity_bf16[:])
-                nc.vector.tensor_copy(table_cols[:, b * LANES : (b + TURNS_A_BANK) * LANES], turned[:])
+                nc.vector.tensor_copy(table_cols[:, b * LANES : (b + TURNS_A_LOAD) * LANES], turned[:])
 
         bias_turned = psum.tile([LANES, LANES], F32, name="bias_turned", tag="bank")
         nc.tensor.transpose(bias_turned[:], bias_rows[:], identity_f32[:])

@@ -20,7 +20,7 @@ BLOCKS_A_PIECE = PIECE // LANES
 TURNS_A_LOAD = 4
 PSUM_BANKS = 8
 DIST_TILES = 16
-ROWS_A_STORE = 2
+ROWS_A_STORE = 1
 
 FLOPS = 2 * N * (FEAT * HID1 + HID1 * HID2 + HID2 * CODE + N * CODE)
 

import concourse.mybir as mybir
from concourse.masks import make_identity

BF16, F32, U16 = mybir.dt.bfloat16, mybir.dt.float32, mybir.dt.uint16
FUNC = mybir.ActivationFunctionType
ALU = mybir.AluOpType

LANES = 128
STORE = 4096
FEAT = 128
HID1, HID2, CODE = 512, 512, 256
N = 2048
PIECE = 512
EPS = 1e-12

PIECES = N // PIECE
ROW_BLOCKS = N // LANES
STORE_BLOCKS = STORE // LANES
BLOCKS_A_PIECE = PIECE // LANES
TURNS_A_LOAD = 4
PSUM_BANKS = 8
DIST_TILES = 16
ROWS_A_STORE = 1

FLOPS = 2 * N * (FEAT * HID1 + HID1 * HID2 + HID2 * CODE + N * CODE)


def tile_controencodnet_b_kernel(tc, table, w1, b1, w2, b2, w3, b3, path_forces, offs, out):
    nc = tc.nc
    with (
        tc.tile_pool(name="held", bufs=1) as held,
        tc.tile_pool(name="weighting", bufs=1) as weighting,
        tc.psum_pool(name="psum", bufs=PSUM_BANKS) as psum,
    ):
        offsets = held.tile([LANES, N // 16], U16, name="offsets")

        identity_bf16 = held.tile([LANES, LANES], BF16, name="identity_bf16")
        make_identity(nc, identity_bf16[:])
        identity_f32 = held.tile([LANES, LANES], F32, name="identity_f32")
        make_identity(nc, identity_f32[:])
        ones_f32 = held.tile([LANES, LANES], F32, name="ones_f32")
        nc.vector.memset(ones_f32[:], 1.0)
        eps_col = held.tile([LANES, 1], F32, name="eps_col")
        nc.vector.memset(eps_col[:], EPS)

        table_cols = held.tile([FEAT, STORE], BF16, name="table_cols")
        w1_sb = held.tile([FEAT, HID1], BF16, name="w1_sb")
        w2_sb = held.tile([LANES, HID1 // LANES, HID2], BF16, name="w2_sb")
        w3_sb = held.tile([LANES, HID2 // LANES, CODE], BF16, name="w3_sb")
        bias_rows = held.tile([LANES, LANES], F32, name="bias_rows")
        bias_cols = held.tile([LANES, 10], F32, name="bias_cols")
        h1 = held.tile([LANES, HID1 // LANES, N], BF16, name="h1")
        feats = held.tile([LANES, CODE // LANES, N], BF16, name="feats")
        sq_row = held.tile([LANES, N], F32, name="sq_row")
        sq_col_less_eps = held.tile([LANES, ROW_BLOCKS], F32, name="sq_col_less_eps")

        with tc.tile_pool(name="loading", bufs=1) as loading:
            table_rows = loading.tile([LANES, STORE_BLOCKS, FEAT], BF16, name="table_rows")
            table_blocks = table.rearrange("(b p) d -> p b d", p=LANES)
            for b in range(0, STORE_BLOCKS, TURNS_A_LOAD):
                nc.sync.dma_start(table_rows[:, b : b + TURNS_A_LOAD, :], table_blocks[:, b : b + TURNS_A_LOAD, :])
            nc.sync.dma_start(offsets[:], offs)
            nc.sync.dma_start(w1_sb[:], w1)
            nc.vector.memset(bias_rows[:], 0.0)
            nc.sync.dma_start(bias_rows[0:4, :], b1.rearrange("(k p) one -> k (p one)", p=LANES))
            nc.sync.dma_start(bias_rows[4:8, :], b2.rearrange("(k p) one -> k (p one)", p=LANES))
            nc.sync.dma_start(bias_rows[8:10, :], b3.rearrange("(k p) one -> k (p one)", p=LANES))
            nc.sync.dma_start(w2_sb[:], w2.rearrange("(k p) n -> p k n", p=LANES))
            nc.sync.dma_start(w3_sb[:], w3.rearrange("(k p) n -> p k n", p=LANES))
            path_all = weighting.tile([LANES, ROW_BLOCKS, N], F32, name="path_all")
            out_blocks = out.rearrange("(r p) j -> p r j", p=LANES)
            for r in range(ROW_BLOCKS):
                path = path_all[:, r, :]
                nc.sync.dma_start(path, path_forces[r * LANES : (r + 1) * LANES, :])
                nc.gpsimd.affine_select(
                    out=path[:, r * LANES : (r + 1) * LANES],
                    in_=path[:, r * LANES : (r + 1) * LANES],
                    compare_op=ALU.not_equal,
                    fill=0.0,
                    base=0,
                    pattern=[[-1, LANES]],
                    channel_multiplier=1,
                )

            for b in range(0, STORE_BLOCKS, TURNS_A_LOAD):
                turned = psum.tile([LANES, TURNS_A_LOAD * LANES], BF16, name="turned", tag="bank")
                for t in range(TURNS_A_LOAD):
                    nc.tensor.transpose(turned[:, t * LANES : (t + 1) * LANES], table_rows[:, b + t, :], identity_bf16[:])
                nc.vector.tensor_copy(table_cols[:, b * LANES : (b + TURNS_A_LOAD) * LANES], turned[:])

        bias_turned = psum.tile([LANES, LANES], F32, name="bias_turned", tag="bank")
        nc.tensor.transpose(bias_turned[:], bias_rows[:], identity_f32[:])
        nc.vector.tensor_copy(bias_cols[:], bias_turned[:, 0:10])
        b1_cols, b2_cols, b3_cols = bias_cols[:, 0:4], bias_cols[:, 4:8], bias_cols[:, 8:10]

        for c in range(PIECES):
            cols = slice(c * PIECE, (c + 1) * PIECE)
            looked_up = table_cols[:].indirect(offsets[:, c * (PIECE // 16) : (c + 1) * (PIECE // 16)])
            for m in range(HID1 // LANES):
                acc = psum.tile([LANES, PIECE], F32, name="acc", tag="bank")
                nc.tensor.matmul(acc[:], w1_sb[:, m * LANES : (m + 1) * LANES], looked_up, start=True, stop=True)
                nc.scalar.activation(h1[:, m, cols], acc[:], FUNC.Tanh, bias=b1_cols[:, m : m + 1])

        with (
            tc.tile_pool(name="hidden", bufs=2) as hidden,
            tc.tile_pool(name="squares", bufs=2) as squares,
            tc.tile_pool(name="distances", bufs=DIST_TILES) as distances,
        ):
            h2_of_piece = {}
            both_of_piece = {}
            dist_of = {}

            def layer2(c):
                cols = slice(c * PIECE, (c + 1) * PIECE)
                h2 = hidden.tile([LANES, HID2 // LANES, PIECE], BF16, name="h2")
                h2_of_piece[c] = h2
                for m in range(HID2 // LANES):
                    acc = psum.tile([LANES, PIECE], F32, name="acc", tag="bank")
                    for k in range(HID1 // LANES):
                        nc.tensor.matmul(
                            acc[:],
                            w2_sb[:, k, m * LANES : (m + 1) * LANES],
                            h1[:, k, cols],
                            start=(k == 0),
                            stop=(k == HID1 // LANES - 1),
                        )
                    nc.scalar.activation(h2[:, m, :], acc[:], FUNC.Tanh, bias=b2_cols[:, m : m + 1])

            def layer3(c):
                cols = slice(c * PIECE, (c + 1) * PIECE)
                h2 = h2_of_piece[c]
                squared = squares.tile([LANES, CODE // LANES, PIECE], F32, name="squared")
                for m in range(CODE // LANES):
                    acc = psum.tile([LANES, PIECE], F32, name="acc", tag="bank")
                    for k in range(HID2 // LANES):
                        nc.tensor.matmul(
                            acc[:],
                            w3_sb[:, k, m * LANES : (m + 1) * LANES],
                            h2[:, k, :],
                            start=(k == 0),
                            stop=(k == HID2 // LANES - 1),
                        )
                    nc.scalar.activation(feats[:, m, cols], acc[:], FUNC.Sigmoid, bias=b3_cols[:, m : m + 1])
                    nc.vector.tensor_tensor(squared[:, m, :], feats[:, m, cols], feats[:, m, cols], ALU.mult)
                both = squares.tile([LANES, PIECE], F32, name="both")
                nc.vector.tensor_tensor(both[:], squared[:, 0, :], squared[:, 1, :], ALU.add)
                both_of_piece[c] = both

            def sum_squares(c):
                cols = slice(c * PIECE, (c + 1) * PIECE)
                summed = psum.tile([LANES, PIECE], F32, name="summed", tag="bank")
                nc.tensor.matmul(summed[:], ones_f32[:], both_of_piece[c][:], start=True, stop=True)
                nc.vector.tensor_copy(sq_row[:, cols], summed[:])

            def squares_as_columns(c):
                blocks = slice(c * BLOCKS_A_PIECE, (c + 1) * BLOCKS_A_PIECE)
                sq_turned = psum.tile([LANES, BLOCKS_A_PIECE, LANES], F32, name="sq_turned", tag="bank")
                for b in range(BLOCKS_A_PIECE):
                    r = c * BLOCKS_A_PIECE + b
                    nc.tensor.transpose(sq_turned[:, b, :], sq_row[:, r * LANES : (r + 1) * LANES], identity_f32[:])
                nc.vector.tensor_scalar_sub(sq_col_less_eps[:, blocks].unsqueeze(2), sq_turned[:, :, 0:1], EPS)

            def row_blocks_of(piece):
                return range(piece * BLOCKS_A_PIECE, (piece + 1) * BLOCKS_A_PIECE)

            def clamp(r, c):
                lo, hi = max(r * LANES, c * PIECE), (c + 1) * PIECE
                width = hi - lo
                dots = psum.tile([LANES, PIECE], F32, name="dots", tag="bank")
                for k in range(CODE // LANES):
                    nc.tensor.matmul(
                        dots[:, :width],
                        feats[:, k, r * LANES : (r + 1) * LANES],
                        feats[:, k, lo:hi],
                        start=(k == 0),
                        stop=(k == CODE // LANES - 1),
                    )
                dist = distances.tile([LANES, PIECE], F32, name="dist")
                dist_of[(r, c)] = (dist, lo)
                nc.vector.scalar_tensor_tensor(
                    out=dist[:, :width],
                    in0=dots[:, :width],
                    scalar=-2.0,
                    in1=sq_row[:, lo:hi],
                    op0=ALU.mult,
                    op1=ALU.add,
                )
                nc.scalar.activation(dist[:, :width], dist[:, :width], FUNC.Relu, bias=sq_col_less_eps[:, r : r + 1])

            def root(r, c):
                dist, lo = dist_of[(r, c)]
                width = (c + 1) * PIECE - lo
                nc.scalar.activation(dist[:, :width], dist[:, :width], FUNC.Sqrt, bias=eps_col[:])

            def roots(a, c, clamped=0):
                for n, r in enumerate(row_blocks_of(a)):
                    if n >= clamped:
                        clamp(r, c)
                    root(r, c)

            def direct_products(a, c):
                for r in row_blocks_of(a):
                    dist, first = dist_of[(r, c)]
                    lo, hi = max((r + 1) * LANES, c * PIECE), (c + 1) * PIECE
                    if lo < hi:
                        nc.gpsimd.tensor_tensor(path_all[:, r, lo:hi], dist[:, lo - first : hi - first], path_all[:, r, lo:hi], ALU.mult)
                    if a < c and (r + 1) % ROWS_A_STORE == 0:
                        store(slice(r + 1 - ROWS_A_STORE, r + 1), c)

            def mirrored_products(a, c):
                for r in row_blocks_of(c):
                    sources = [s for s in row_blocks_of(a) if s <= r]
                    lo, hi = a * PIECE, a * PIECE + len(sources) * LANES
                    turned_back = psum.tile([LANES, PIECE], F32, name="turned_back", tag="bank")
                    for s in sources:
                        dist, first = dist_of[(s, c)]
                        nc.tensor.transpose(
                            turned_back[:, s * LANES - lo : (s + 1) * LANES - lo],
                            dist[:, r * LANES - first : (r + 1) * LANES - first],
                            identity_f32[:],
                        )
                    nc.vector.tensor_tensor(path_all[:, r, lo:hi], turned_back[:, : hi - lo], path_all[:, r, lo:hi], ALU.mult)
                    if a == c:
                        store(slice(r, r + 1), a)
                    elif (r + 1) % ROWS_A_STORE == 0:
                        store(slice(r + 1 - ROWS_A_STORE, r + 1), a)

            def store(blocks, piece):
                cols = slice(piece * PIECE, (piece + 1) * PIECE)
                nc.sync.dma_start(out_blocks[:, blocks, cols], path_all[:, blocks, cols])

            def finish(a, c):
                direct_products(a, c)
                mirrored_products(a, c)

            layer2(0)
            layer2(1)
            layer3(0)
            layer2(2)
            layer3(1)
            sum_squares(0)
            layer2(3)
            squares_as_columns(0)
            layer3(2)
            sum_squares(1)
            squares_in_order = [(a, c) for c in range(PIECES) for a in range(c)] + [(c, c) for c in range(PIECES)]
            first_a, first_c = squares_in_order[0]
            clamp(row_blocks_of(first_a)[0], first_c)
            layer3(3)
            roots(first_a, first_c, clamped=1)
            squares_as_columns(1)
            sum_squares(2)
            roots(*squares_in_order[1])
            finish(*squares_in_order[0])
            sum_squares(3)
            squares_as_columns(2)
            roots(*squares_in_order[2])
            finish(*squares_in_order[1])
            squares_as_columns(3)
            for n in range(3, len(squares_in_order)):
                roots(*squares_in_order[n])
                finish(*squares_in_order[n - 1])
            finish(*squares_in_order[-1])
